import numpy as np
import ml_dtypes


def mxq(x, axis, fmt="e4m3"):
    dtype, down = {"e4m3": (ml_dtypes.float8_e4m3fn, 7), "e5m2": (ml_dtypes.float8_e5m2, 14)}[fmt]
    v = np.moveaxis(np.asarray(x, np.float32).astype(ml_dtypes.bfloat16).astype(np.float64), axis, -1)
    blocks = v.reshape(v.shape[:-1] + (-1, 32))
    amax = np.abs(blocks).max(-1, keepdims=True)
    byte = np.maximum(np.where(amax > 0, np.frexp(amax)[1] - 1 + 127, 0) - down, 1)
    scale = np.exp2(byte - 127.0)
    codes = (blocks / scale).astype(np.float32).astype(dtype).astype(np.float64)
    return np.moveaxis((codes * scale).reshape(v.shape), -1, axis)


WIDE = False


def mx_kscale(k):
    if not WIDE:
        return np.ones(k)
    levels = np.array([10, -10, 5, -5, 0])
    a = np.random.permutation(np.resize(levels, k // 512 * 4)).reshape(k // 512, 4)
    idx = np.arange(k)
    return np.exp2(a[idx // 512, idx % 128 // 32])


BF16 = ml_dtypes.bfloat16


def bf(x):
    return np.asarray(x, np.float32).astype(BF16)


def f64(x):
    return np.asarray(x).astype(np.float64)


B, H, L, D, C = 1, 8, 2048, 128, 512


def decay_block(i0, n):
    head_idx = np.arange(H, dtype=np.float64)
    gamma = 1.0 - np.exp2(-5.0 - head_idx)
    log2_gamma = np.log2(gamma)
    pos_diff = np.arange(i0, i0 + C, dtype=np.float64)[:, None] - np.arange(n, dtype=np.float64)[None, :]
    causal = np.where(pos_diff >= 0, 1.0, 0.0)
    return np.exp2(pos_diff[None] * log2_gamma[:, None, None]) * causal[None]


def setup_inputs():
    s = mx_kscale(L)
    return {"q_scaled": bf(np.random.standard_normal((B, H, L, D)) / np.sqrt(D)),
            "k": bf(np.random.standard_normal((B, H, L, D)) * s[:, None]),
            "v": bf(np.random.standard_normal((B, H, L, D)) * 0.25 / s[:, None])}


def reference(q_scaled, k, v):
    vq = mxq(f64(v), 2, "e4m3")
    out = np.zeros((B, H, L, D))
    for i0 in range(0, L, C):
        n = i0 + C
        scores = f64(q_scaled)[:, :, i0:n] @ f64(k)[:, :, :n].transpose(0, 1, 3, 2)
        p = scores * decay_block(i0, n)[None]
        out[:, :, i0:n] = mxq(p, 3, "e4m3") @ vq[:, :, :n]
    return out

@@ -1,0 +1,203 @@
+import math
+from contextlib import ExitStack
+
+import concourse.mybir as mybir
+from concourse.masks import make_identity
+
+BF16 = mybir.dt.bfloat16
+F32 = mybir.dt.float32
+I32 = mybir.dt.int32
+U32 = mybir.dt.uint32
+U8 = mybir.dt.uint8
+FP8X4 = mybir.dt.float8_e4m3fn_x4
+MULT = mybir.AluOpType.mult
+
+HEADS = 8
+SEQ = 2048
+D = 128
+P = 128
+PACK = 4
+CHUNK = P * PACK
+N_CHUNKS = SEQ // CHUNK
+BLOCKS = SEQ // P
+
+SHIFT = (PACK - 1) * P
+
+FLOPS = 2 * 2 * HEADS * D * sum(CHUNK * CHUNK * (r + 1) for r in range(N_CHUNKS))
+
+
+def tile_model_pa_kernel(tc, q_scaled, k, v, out):
+    nc = tc.nc
+    gammas = [1.0 - 2.0 ** (-5 - h) for h in range(HEADS)]
+
+    with ExitStack() as ctx:
+        ctx.enter_context(tc.manual_schedule())
+        const = ctx.enter_context(tc.tile_pool(name="const", bufs=1))
+        raw = ctx.enter_context(tc.tile_pool(name="raw", bufs=HEADS))
+        per_head = ctx.enter_context(tc.tile_pool(name="per_head", bufs=2))
+        per_chunk = ctx.enter_context(tc.tile_pool(name="per_chunk", bufs=2))
+        work = ctx.enter_context(tc.tile_pool(name="work", bufs=3))
+        psum_scores = ctx.enter_context(tc.psum_pool(name="psum_scores", bufs=4))
+        psum_t = ctx.enter_context(tc.psum_pool(name="psum_t", bufs=2))
+        psum_out = ctx.enter_context(tc.psum_pool(name="psum_out", bufs=2))
+
+        k_raw, q_raw, v_raw = [], [], []
+        for h in range(HEADS):
+            for source, tiles, label in ((k, k_raw, "k_raw"), (q_scaled, q_raw, "q_raw"), (v, v_raw, "v_raw")):
+                rows = raw.tile([P, BLOCKS, D], BF16, name=label)
+                nc.sync.dma_start(out=rows[:], in_=source[0, h].rearrange("(b p) d -> p b d", p=P))
+                tiles.append(rows)
+
+        exponent_pattern = [[1, P], [-P, PACK]]
+        exponent_i32 = const.tile([P, P, PACK], I32)
+        nc.gpsimd.iota(exponent_i32[:], pattern=exponent_pattern, base=SHIFT, channel_multiplier=-1)
+        exponent = const.tile([P, P, PACK], F32)
+        nc.vector.tensor_copy(out=exponent[:], in_=exponent_i32[:])
+        identity = const.tile([P, P], BF16)
+        make_identity(nc, identity[:])
+        diagonal_tiles = []
+        for i in range(2):
+            zeroed = const.tile([P, PACK, P, PACK], BF16, name="diagonal%d" % i, align_bytes=64)
+            nc.vector.memset(zeroed[:], 0.0)
+            diagonal_tiles.append(zeroed)
+
+        k_t, q_t, decay, causal, v_grouped, v_codes, v_scales = {}, {}, {}, {}, {}, {}, {}
+        p_codes, p_scales, p_grouped = {}, {}, {}
+
+        def transpose_chunk(rows, transposed, c):
+            flipped = psum_t.tile([P, PACK, P], BF16)
+            for b in range(PACK):
+                nc.tensor.transpose(out=flipped[:, b, :], in_=rows[:, PACK * c + b, :], identity=identity[:])
+            nc.scalar.copy(
+                out=transposed[:, c * CHUNK : (c + 1) * CHUNK], in_=flipped[:].rearrange("p b x -> p (b x)")
+            )
+
+        def start_head(h):
+            k_t[h] = per_head.tile([P, SEQ], BF16, name="k_t")
+            q_t[h] = per_head.tile([P, SEQ], BF16, name="q_t")
+            decay[h] = per_head.tile([P, P, PACK], F32, name="decay")
+            nc.scalar.activation(
+                out=decay[h][:],
+                in_=exponent[:],
+                func=mybir.ActivationFunctionType.Exp,
+                scale=math.log(gammas[h]),
+            )
+            causal[h] = per_head.tile([P, P, PACK], F32, name="causal")
+            nc.gpsimd.affine_select(
+                out=causal[h][:],
+                in_=decay[h][:],
+                pattern=exponent_pattern,
+                compare_op=mybir.AluOpType.is_ge,
+                fill=0.0,
+                base=SHIFT,
+                channel_multiplier=-1,
+            )
+
+        def regroup_v(h):
+            v_grouped[h] = per_head.tile([P, N_CHUNKS, D, PACK], BF16, name="v_grouped", align_bytes=64)
+            nc.scalar.copy(out=v_grouped[h][:], in_=v_raw[h][:].rearrange("p (g t) d -> p g d t", t=PACK))
+
+        def quantise_v(h):
+            v_codes[h] = per_head.tile([P, N_CHUNKS, D], U32, name="v_codes", align_bytes=64)
+            v_scales[h] = per_head.tile([P, N_CHUNKS, D], U8, name="v_scales", align_bytes=64)
+            nc.vector.quantize_mx(
+                out=v_codes[h][:].rearrange("p g d -> p (g d)").bitcast(FP8X4),
+                scales=v_scales[h][:].rearrange("p g d -> p (g d)"),
+                in_=v_grouped[h][:].rearrange("p g d t -> p (g d t)"),
+            )
+
+        def decayed_scores(h, r, g):
+            diagonal = g == r
+            if diagonal:
+                grouped = diagonal_tiles[r % 2]
+            else:
+                grouped = work.tile([P, PACK, P, PACK], BF16, name="grouped", align_bytes=64)
+            for b in range(PACK):
+                key_blocks = b + 1 if diagonal else PACK
+                scores_t = psum_scores.tile([P, PACK, P], F32)
+                for t in range(key_blocks):
+                    key_block = PACK * g + t
+                    query_block = PACK * r + b
+                    nc.tensor.matmul(
+                        out=scores_t[:, t, :],
+                        lhsT=k_t[h][:, key_block * P : (key_block + 1) * P],
+                        rhs=q_t[h][:, query_block * P : (query_block + 1) * P],
+                        start=True,
+                        stop=True,
+                    )
+                by_query = scores_t[:, 0:key_blocks, :].rearrange("p t i -> p i t")
+                if diagonal:
+                    nc.vector.tensor_tensor(
+                        out=grouped[:, b, :, 0:key_blocks],
+                        in0=by_query,
+                        in1=causal[h][:, :, PACK - key_blocks : PACK],
+                        op=MULT,
+                    )
+                else:
+                    distance = CHUNK * (r - g) + P * b
+                    nc.vector.scalar_tensor_tensor(
+                        out=grouped[:, b, :, :],
+                        in0=by_query,
+                        scalar=gammas[h] ** (distance - SHIFT),
+                        in1=decay[h][:],
+                        op0=MULT,
+                        op1=MULT,
+                    )
+            return grouped
+
+        def quantise_scores(h, r, g, grouped):
+            if g == 0:
+                p_codes[h, r] = per_chunk.tile([P, N_CHUNKS, CHUNK], U32, name="p_codes", align_bytes=64)
+                p_scales[h, r] = per_chunk.tile([P, N_CHUNKS, CHUNK], U8, name="p_scales", align_bytes=64)
+            nc.vector.quantize_mx(
+                out=p_codes[h, r][:, g, :].bitcast(FP8X4),
+                scales=p_scales[h, r][:, g, :],
+                in_=grouped[:].rearrange("p b i t -> p (b i t)"),
+            )
+
+        def weighted_values(h, r):
+            acc = psum_out.tile([P, PACK, D], F32)
+            for b in range(PACK):
+                queries = slice(b * P, (b + 1) * P)
+                for g in range(r + 1):
+                    nc.tensor.matmul_mx(
+                        out=acc[:, b, :],
+                        lhsT=p_codes[h, r][:, g, queries].bitcast(FP8X4),
+                        lhsT_scale=p_scales[h, r][:, g, queries],
+                        rhs=v_codes[h][:, g, :].bitcast(FP8X4),
+                        rhs_scale=v_scales[h][:, g, :],
+                        start=(g == 0),
+                        stop=(g == r),
+                    )
+            result = work.tile([P, PACK, D], F32)
+            nc.scalar.copy(out=result[:], in_=acc[:])
+            nc.sync.dma_start(
+                out=out[0, h, r * CHUNK : (r + 1) * CHUNK, :].rearrange("(b p) d -> p b d", p=P), in_=result[:]
+            )
+
+        def prepare_chunk(h, r):
+            if r == 0:
+                start_head(h)
+            transpose_chunk(k_raw[h], k_t[h], r)
+            transpose_chunk(q_raw[h], q_t[h], r)
+            if r == 0:
+                regroup_v(h)
+
+        chunks = [(h, r) for h in range(HEADS) for r in range(N_CHUNKS)]
+        batches = [(h, r, g) for (h, r) in chunks for g in range(r + 1)]
+        prepare_chunk(0, 0)
+        for n in range(len(batches) + 2):
+            if n < len(batches):
+                h, r, g = batches[n]
+                following = chunks.index((h, r)) + 1
+                if g == 0 and following < len(chunks):
+                    prepare_chunk(*chunks[following])
+                p_grouped[n] = decayed_scores(h, r, g)
+                if r == 0:
+                    quantise_v(h)
+            if 1 <= n <= len(batches):
+                quantise_scores(*batches[n - 1], p_grouped[n - 1])
+            if n >= 2:
+                h, r, g = batches[n - 2]
+                if g == r:
+                    weighted_values(h, r)

@@ -37,16 +37,29 @@ def tile_model_pa_kernel(tc, q_scaled, k, v, out):
         per_head = ctx.enter_context(tc.tile_pool(name="per_head", bufs=2))
         per_chunk = ctx.enter_context(tc.tile_pool(name="per_chunk", bufs=2))
         work = ctx.enter_context(tc.tile_pool(name="work", bufs=3))
-        psum_scores = ctx.enter_context(tc.psum_pool(name="psum_scores", bufs=4))
+        psum_vector = ctx.enter_context(tc.psum_pool(name="psum_vector", bufs=PACK - 1))
+        psum_scalar = ctx.enter_context(tc.psum_pool(name="psum_scalar", bufs=1))
         psum_t = ctx.enter_context(tc.psum_pool(name="psum_t", bufs=2))
         psum_out = ctx.enter_context(tc.psum_pool(name="psum_out", bufs=2))
 
+        def load(rows, source, h, first_block, n_blocks):
+            nc.sync.dma_start(
+                out=rows[:, first_block : first_block + n_blocks, :],
+                in_=source[0, h, first_block * P : (first_block + n_blocks) * P, :].rearrange(
+                    "(b p) d -> p b d", p=P
+                ),
+            )
+
         k_raw, q_raw, v_raw = [], [], []
         for h in range(HEADS):
-            for source, tiles, label in ((k, k_raw, "k_raw"), (q_scaled, q_raw, "q_raw"), (v, v_raw, "v_raw")):
-                rows = raw.tile([P, BLOCKS, D], BF16, name=label)
-                nc.sync.dma_start(out=rows[:], in_=source[0, h].rearrange("(b p) d -> p b d", p=P))
-                tiles.append(rows)
+            k_raw.append(raw.tile([P, BLOCKS, D], BF16, name="k_raw"))
+            q_raw.append(raw.tile([P, BLOCKS, D], BF16, name="q_raw"))
+            v_raw.append(raw.tile([P, BLOCKS, D], BF16, name="v_raw"))
+            for c in range(N_CHUNKS):
+                load(k_raw[h], k, h, PACK * c, PACK)
+                load(q_raw[h], q_scaled, h, PACK * c, PACK)
+                if c == 1:
+                    load(v_raw[h], v, h, 0, BLOCKS)
 
         exponent_pattern = [[1, P], [-P, PACK]]
         exponent_i32 = const.tile([P, P, PACK], I32)
@@ -75,6 +88,7 @@ def tile_model_pa_kernel(tc, q_scaled, k, v, out):
         def start_head(h):
             k_t[h] = per_head.tile([P, SEQ], BF16, name="k_t")
             q_t[h] = per_head.tile([P, SEQ], BF16, name="q_t")
+            v_grouped[h] = per_head.tile([P, N_CHUNKS, D, PACK], BF16, name="v_grouped", align_bytes=64)
             decay[h] = per_head.tile([P, P, PACK], F32, name="decay")
             nc.scalar.activation(
                 out=decay[h][:],
@@ -93,9 +107,11 @@ def tile_model_pa_kernel(tc, q_scaled, k, v, out):
                 channel_multiplier=-1,
             )
 
-        def regroup_v(h):
-            v_grouped[h] = per_head.tile([P, N_CHUNKS, D, PACK], BF16, name="v_grouped", align_bytes=64)
-            nc.scalar.copy(out=v_grouped[h][:], in_=v_raw[h][:].rearrange("p (g t) d -> p g d t", t=PACK))
+        def regroup_v(h, g):
+            nc.scalar.copy(
+                out=v_grouped[h][:, g, :, :],
+                in_=v_raw[h][:, PACK * g : PACK * (g + 1), :].rearrange("p t d -> p d t"),
+            )
 
         def quantise_v(h):
             v_codes[h] = per_head.tile([P, N_CHUNKS, D], U32, name="v_codes", align_bytes=64)
@@ -113,8 +129,10 @@ def tile_model_pa_kernel(tc, q_scaled, k, v, out):
             else:
                 grouped = work.tile([P, PACK, P, PACK], BF16, name="grouped", align_bytes=64)
             for b in range(PACK):
+                through_scalar = b == PACK - 1
                 key_blocks = b + 1 if diagonal else PACK
-                scores_t = psum_scores.tile([P, PACK, P], F32)
+                bank = psum_scalar if through_scalar else psum_vector
+                scores_t = bank.tile([P, PACK, P], F32, name="scores_t")
                 for t in range(key_blocks):
                     key_block = PACK * g + t
                     query_block = PACK * r + b
@@ -127,19 +145,23 @@ def tile_model_pa_kernel(tc, q_scaled, k, v, out):
                     )
                 by_query = scores_t[:, 0:key_blocks, :].rearrange("p t i -> p i t")
                 if diagonal:
-                    nc.vector.tensor_tensor(
+                    table = causal[h][:, :, PACK - key_blocks : PACK]
+                    factor = 1.0
+                else:
+                    table = decay[h][:]
+                    factor = gammas[h] ** (CHUNK * (r - g) + P * b - SHIFT)
+                if through_scalar:
+                    staged = work.tile([P, P, PACK], F32)
+                    nc.scalar.activation(
+                        out=staged[:], in_=by_query, func=mybir.ActivationFunctionType.Copy, scale=factor
+                    )
+                    nc.gpsimd.tensor_tensor(out=grouped[:, b, :, :], in0=staged[:], in1=table, op=MULT)
+                else:
+                    nc.vector.scalar_tensor_tensor(
                         out=grouped[:, b, :, 0:key_blocks],
                         in0=by_query,
-                        in1=causal[h][:, :, PACK - key_blocks : PACK],
-                        op=MULT,
-                    )
-                else:
-                    distance = CHUNK * (r - g) + P * b
-                    nc.vector.scalar_tensor_tensor(
-                        out=grouped[:, b, :, :],
-                        in0=by_query,
-                        scalar=gammas[h] ** (distance - SHIFT),
-                        in1=decay[h][:],
+                        scalar=factor,
+                        in1=table,
                         op0=MULT,
                         op1=MULT,
                     )
@@ -171,7 +193,7 @@ def tile_model_pa_kernel(tc, q_scaled, k, v, out):
                     )
             result = work.tile([P, PACK, D], F32)
             nc.scalar.copy(out=result[:], in_=acc[:])
-            nc.sync.dma_start(
+            nc.scalar.dma_start(
                 out=out[0, h, r * CHUNK : (r + 1) * CHUNK, :].rearrange("(b p) d -> p b d", p=P), in_=result[:]
             )
 
@@ -180,8 +202,6 @@ def tile_model_pa_kernel(tc, q_scaled, k, v, out):
                 start_head(h)
             transpose_chunk(k_raw[h], k_t[h], r)
             transpose_chunk(q_raw[h], q_t[h], r)
-            if r == 0:
-                regroup_v(h)
 
         chunks = [(h, r) for h in range(HEADS) for r in range(N_CHUNKS)]
         batches = [(h, r, g) for (h, r) in chunks for g in range(r + 1)]
@@ -189,11 +209,16 @@ def tile_model_pa_kernel(tc, q_scaled, k, v, out):
         for n in range(len(batches) + 2):
             if n < len(batches):
                 h, r, g = batches[n]
+                p_grouped[n] = decayed_scores(h, r, g)
                 following = chunks.index((h, r)) + 1
                 if g == 0 and following < len(chunks):
                     prepare_chunk(*chunks[following])
-                p_grouped[n] = decayed_scores(h, r, g)
-                if r == 0:
+                if n == 0:
+                    for key_chunk in range(N_CHUNKS):
+                        regroup_v(0, key_chunk)
+                if r == N_CHUNKS - 1 and h + 1 < HEADS:
+                    regroup_v(h + 1, g)
+                if (r, g) == (1, 0):
                     quantise_v(h)
             if 1 <= n <= len(batches):
                 quantise_scores(*batches[n - 1], p_grouped[n - 1])

@@ -128,7 +128,7 @@ def tile_model_pa_kernel(tc, q_scaled, k, v, out):
                 grouped = diagonal_tiles[r % 2]
             else:
                 grouped = work.tile([P, PACK, P, PACK], BF16, name="grouped", align_bytes=64)
-            for b in range(PACK):
+            for b in (0, PACK - 1, 1, 2):
                 through_scalar = b == PACK - 1
                 key_blocks = b + 1 if diagonal else PACK
                 bank = psum_scalar if through_scalar else psum_vector

@@ -11,6 +11,8 @@ U32 = mybir.dt.uint32
 U8 = mybir.dt.uint8
 FP8X4 = mybir.dt.float8_e4m3fn_x4
 MULT = mybir.AluOpType.mult
+COPY = mybir.ActivationFunctionType.Copy
+EXP = mybir.ActivationFunctionType.Exp
 
 HEADS = 8
 SEQ = 2048
@@ -22,6 +24,8 @@ N_CHUNKS = SEQ // CHUNK
 BLOCKS = SEQ // P
 
 SHIFT = (PACK - 1) * P
+N_DISTANCES = BLOCKS - PACK
+LOOKAHEAD = 2
 
 FLOPS = 2 * 2 * HEADS * D * sum(CHUNK * CHUNK * (r + 1) for r in range(N_CHUNKS))
 
@@ -35,12 +39,10 @@ def tile_model_pa_kernel(tc, q_scaled, k, v, out):
         const = ctx.enter_context(tc.tile_pool(name="const", bufs=1))
         raw = ctx.enter_context(tc.tile_pool(name="raw", bufs=HEADS))
         per_head = ctx.enter_context(tc.tile_pool(name="per_head", bufs=2))
-        per_chunk = ctx.enter_context(tc.tile_pool(name="per_chunk", bufs=2))
+        per_chunk = ctx.enter_context(tc.tile_pool(name="per_chunk", bufs=3))
         work = ctx.enter_context(tc.tile_pool(name="work", bufs=3))
-        psum_vector = ctx.enter_context(tc.psum_pool(name="psum_vector", bufs=PACK - 1))
-        psum_scalar = ctx.enter_context(tc.psum_pool(name="psum_scalar", bufs=1))
-        psum_t = ctx.enter_context(tc.psum_pool(name="psum_t", bufs=2))
-        psum_out = ctx.enter_context(tc.psum_pool(name="psum_out", bufs=2))
+        psum_vector = ctx.enter_context(tc.psum_pool(name="psum_vector", bufs=3))
+        psum_scalar = ctx.enter_context(tc.psum_pool(name="psum_scalar", bufs=5))
 
         def load(rows, source, h, first_block, n_blocks):
             nc.sync.dma_start(
@@ -61,51 +63,66 @@ def tile_model_pa_kernel(tc, q_scaled, k, v, out):
                 if c == 1:
                     load(v_raw[h], v, h, 0, BLOCKS)
 
-        exponent_pattern = [[1, P], [-P, PACK]]
-        exponent_i32 = const.tile([P, P, PACK], I32)
-        nc.gpsimd.iota(exponent_i32[:], pattern=exponent_pattern, base=SHIFT, channel_multiplier=-1)
-        exponent = const.tile([P, P, PACK], F32)
-        nc.vector.tensor_copy(out=exponent[:], in_=exponent_i32[:])
+        def exponents(shape, pattern, base, channel_multiplier, label):
+            as_i32 = const.tile(shape, I32, name=label + "_i32")
+            nc.gpsimd.iota(as_i32[:], pattern=pattern, base=base, channel_multiplier=channel_multiplier)
+            as_f32 = const.tile(shape, F32, name=label)
+            nc.vector.tensor_copy(out=as_f32[:], in_=as_i32[:])
+            return as_f32
+
+        table_pattern = [[1, P], [-P, PACK]]
+        table_exponent = exponents([P, P, PACK], table_pattern, SHIFT, -1, "table_exponent")
+        query_exponent = exponents([P, PACK], [[-P, PACK]], SHIFT, 1, "query_exponent")
+        key_exponent = exponents([P, N_DISTANCES], [[P, N_DISTANCES]], P, -1, "key_exponent")
         identity = const.tile([P, P], BF16)
         make_identity(nc, identity[:])
+        identity_f32 = const.tile([P, P], F32)
+        make_identity(nc, identity_f32[:])
         diagonal_tiles = []
         for i in range(2):
             zeroed = const.tile([P, PACK, P, PACK], BF16, name="diagonal%d" % i, align_bytes=64)
             nc.vector.memset(zeroed[:], 0.0)
             diagonal_tiles.append(zeroed)
 
-        k_t, q_t, decay, causal, v_grouped, v_codes, v_scales = {}, {}, {}, {}, {}, {}, {}
-        p_codes, p_scales, p_grouped = {}, {}, {}
+        k_t, q_t, decay, causal, query_factor, key_factor = {}, {}, {}, {}, {}, {}
+        v_grouped, v_codes, v_scales, p_codes, p_scales = {}, {}, {}, {}, {}
 
         def transpose_chunk(rows, transposed, c):
-            flipped = psum_t.tile([P, PACK, P], BF16)
+            flipped = psum_scalar.tile([P, PACK, P], BF16, tag="bank")
             for b in range(PACK):
                 nc.tensor.transpose(out=flipped[:, b, :], in_=rows[:, PACK * c + b, :], identity=identity[:])
             nc.scalar.copy(
                 out=transposed[:, c * CHUNK : (c + 1) * CHUNK], in_=flipped[:].rearrange("p b x -> p (b x)")
             )
 
+        def power_of_gamma(h, exponent, label):
+            power = per_head.tile(list(exponent.shape), F32, name=label)
+            nc.scalar.activation(out=power[:], in_=exponent[:], func=EXP, scale=math.log(gammas[h]))
+            return power
+
         def start_head(h):
             k_t[h] = per_head.tile([P, SEQ], BF16, name="k_t")
             q_t[h] = per_head.tile([P, SEQ], BF16, name="q_t")
             v_grouped[h] = per_head.tile([P, N_CHUNKS, D, PACK], BF16, name="v_grouped", align_bytes=64)
-            decay[h] = per_head.tile([P, P, PACK], F32, name="decay")
-            nc.scalar.activation(
-                out=decay[h][:],
-                in_=exponent[:],
-                func=mybir.ActivationFunctionType.Exp,
-                scale=math.log(gammas[h]),
-            )
+            decay[h] = power_of_gamma(h, table_exponent, "decay")
+            query_factor[h] = power_of_gamma(h, query_exponent, "query_factor")
+            key_factor[h] = power_of_gamma(h, key_exponent, "key_factor")
             causal[h] = per_head.tile([P, P, PACK], F32, name="causal")
             nc.gpsimd.affine_select(
                 out=causal[h][:],
                 in_=decay[h][:],
-                pattern=exponent_pattern,
+                pattern=table_pattern,
                 compare_op=mybir.AluOpType.is_ge,
                 fill=0.0,
                 base=SHIFT,
                 channel_multiplier=-1,
             )
+
+        def prepare_chunk(h, c):
+            if c == 0:
+                start_head(h)
+            transpose_chunk(k_raw[h], k_t[h], c)
+            transpose_chunk(q_raw[h], q_t[h], c)
 
         def regroup_v(h, g):
             nc.scalar.copy(
@@ -122,53 +139,65 @@ def tile_model_pa_kernel(tc, q_scaled, k, v, out):
                 in_=v_grouped[h][:].rearrange("p g d t -> p (g d t)"),
             )
 
-        def decayed_scores(h, r, g):
+        def block(transposed, index):
+            return transposed[:, index * P : (index + 1) * P]
+
+
+        def vector_block(h, r, g, b, grouped):
             diagonal = g == r
+            key_blocks = b + 1 if diagonal else PACK
+            scores_t = psum_vector.tile([P, PACK, P], F32)
+            for t in range(key_blocks):
+                nc.tensor.matmul(
+                    out=scores_t[:, t, :],
+                    lhsT=block(k_t[h], PACK * g + t),
+                    rhs=block(q_t[h], PACK * r + b),
+                    start=True,
+                    stop=True,
+                )
             if diagonal:
-                grouped = diagonal_tiles[r % 2]
+                table = causal[h][:, :, PACK - key_blocks : PACK]
+                factor = 1.0
             else:
-                grouped = work.tile([P, PACK, P, PACK], BF16, name="grouped", align_bytes=64)
-            for b in (0, PACK - 1, 1, 2):
-                through_scalar = b == PACK - 1
-                key_blocks = b + 1 if diagonal else PACK
-                bank = psum_scalar if through_scalar else psum_vector
-                scores_t = bank.tile([P, PACK, P], F32, name="scores_t")
-                for t in range(key_blocks):
-                    key_block = PACK * g + t
-                    query_block = PACK * r + b
-                    nc.tensor.matmul(
-                        out=scores_t[:, t, :],
-                        lhsT=k_t[h][:, key_block * P : (key_block + 1) * P],
-                        rhs=q_t[h][:, query_block * P : (query_block + 1) * P],
-                        start=True,
-                        stop=True,
-                    )
-                by_query = scores_t[:, 0:key_blocks, :].rearrange("p t i -> p i t")
-                if diagonal:
-                    table = causal[h][:, :, PACK - key_blocks : PACK]
-                    factor = 1.0
-                else:
-                    table = decay[h][:]
-                    factor = gammas[h] ** (CHUNK * (r - g) + P * b - SHIFT)
-                if through_scalar:
-                    staged = work.tile([P, P, PACK], F32)
-                    nc.scalar.activation(
-                        out=staged[:], in_=by_query, func=mybir.ActivationFunctionType.Copy, scale=factor
-                    )
-                    nc.gpsimd.tensor_tensor(out=grouped[:, b, :, :], in0=staged[:], in1=table, op=MULT)
-                else:
-                    nc.vector.scalar_tensor_tensor(
-                        out=grouped[:, b, :, 0:key_blocks],
-                        in0=by_query,
-                        scalar=factor,
-                        in1=table,
-                        op0=MULT,
-                        op1=MULT,
-                    )
-            return grouped
+                table = decay[h][:]
+                factor = gammas[h] ** (CHUNK * (r - g) + P * b - SHIFT)
+            nc.vector.scalar_tensor_tensor(
+                out=grouped[:, b, :, 0:key_blocks],
+                in0=scores_t[:, 0:key_blocks, :].rearrange("p t i -> p i t"),
+                scalar=factor,
+                in1=table,
+                op0=MULT,
+                op1=MULT,
+            )
+
+        def scalar_first_half(h, r, g, t, half_done):
+            scores = psum_scalar.tile([P, PACK, P], F32, tag="bank")
+            for b in range(PACK):
+                nc.tensor.matmul(
+                    out=scores[:, b, :],
+                    lhsT=block(q_t[h], PACK * r + b),
+                    rhs=block(k_t[h], PACK * g + t),
+                    start=True,
+                    stop=True,
+                )
+            nc.scalar.activation(
+                out=half_done[:, t, :, :], in_=scores[:], func=COPY, scale=query_factor[h][:, t : t + 1]
+            )
+
+        def scalar_second_half(h, r, g, b, half_done, grouped):
+            flipped = psum_scalar.tile([P, PACK, P], F32, tag="bank")
+            for t in range(PACK):
+                nc.tensor.transpose(out=flipped[:, t, :], in_=half_done[:, t, b, :], identity=identity_f32[:])
+            m = PACK * (r - g) + b - PACK
+            nc.scalar.activation(
+                out=grouped[:, b, :, :],
+                in_=flipped[:].rearrange("p t i -> p i t"),
+                func=COPY,
+                scale=key_factor[h][:, m : m + 1],
+            )
 
         def quantise_scores(h, r, g, grouped):
-            if g == 0:
+            if (h, r) not in p_codes:
                 p_codes[h, r] = per_chunk.tile([P, N_CHUNKS, CHUNK], U32, name="p_codes", align_bytes=64)
                 p_scales[h, r] = per_chunk.tile([P, N_CHUNKS, CHUNK], U8, name="p_scales", align_bytes=64)
             nc.vector.quantize_mx(
@@ -178,7 +207,7 @@ def tile_model_pa_kernel(tc, q_scaled, k, v, out):
             )
 
         def weighted_values(h, r):
-            acc = psum_out.tile([P, PACK, D], F32)
+            acc = psum_scalar.tile([P, PACK, D], F32, tag="bank")
             for b in range(PACK):
                 queries = slice(b * P, (b + 1) * P)
                 for g in range(r + 1):
@@ -193,36 +222,66 @@ def tile_model_pa_kernel(tc, q_scaled, k, v, out):
                     )
             result = work.tile([P, PACK, D], F32)
             nc.scalar.copy(out=result[:], in_=acc[:])
-            nc.scalar.dma_start(
+            nc.gpsimd.dma_start(
                 out=out[0, h, r * CHUNK : (r + 1) * CHUNK, :].rearrange("(b p) d -> p b d", p=P), in_=result[:]
             )
 
-        def prepare_chunk(h, r):
-            if r == 0:
-                start_head(h)
-            transpose_chunk(k_raw[h], k_t[h], r)
-            transpose_chunk(q_raw[h], q_t[h], r)
+        rounds = []
+        for h in range(HEADS):
+            for_vector = [(r, g) for r in range(N_CHUNKS) for g in range(r + 1) if g > 0 or r == 0]
+            for_scalar = [(r, g) for r in range(N_CHUNKS) for g in range(r + 1) if g == 0 and r > 0]
+            halves = [(r, g, second) for (r, g) in for_scalar for second in (False, True)] + [None]
+            rounds.extend((h, batch, half) for batch, half in zip(for_vector, halves))
 
-        chunks = [(h, r) for h in range(HEADS) for r in range(N_CHUNKS)]
-        batches = [(h, r, g) for (h, r) in chunks for g in range(r + 1)]
-        prepare_chunk(0, 0)
-        for n in range(len(batches) + 2):
-            if n < len(batches):
-                h, r, g = batches[n]
-                p_grouped[n] = decayed_scores(h, r, g)
-                following = chunks.index((h, r)) + 1
-                if g == 0 and following < len(chunks):
-                    prepare_chunk(*chunks[following])
+        def chunks_read(n):
+            if n >= len(rounds):
+                return []
+            h, (r, g), half = rounds[n]
+            return [(h, c) for c in sorted({r, g} | (set(half[0:2]) if half else set()))]
+
+        prepared = []
+        to_quantise = {}
+        batches_left = {(h, r): r + 1 for h in range(HEADS) for r in range(N_CHUNKS)}
+        complete = []
+        half_done = None
+        scalar_grouped = None
+        for n in range(-LOOKAHEAD, len(rounds) + 3):
+            if 0 <= n < len(rounds):
+                h, (r, g), half = rounds[n]
+                if g == r:
+                    grouped = diagonal_tiles[r % 2]
+                else:
+                    grouped = work.tile([P, PACK, P, PACK], BF16, name="grouped", align_bytes=64)
+                if half and not half[2]:
+                    half_done = work.tile([P, PACK, PACK, P], F32, name="half_done", bufs=2)
+                    scalar_grouped = work.tile([P, PACK, P, PACK], BF16, name="scalar_grouped", align_bytes=64)
+                for x in range(PACK):
+                    vector_block(h, r, g, x, grouped)
+                    if half and not half[2]:
+                        scalar_first_half(h, half[0], half[1], x, half_done)
+                    if half and half[2]:
+                        scalar_second_half(h, half[0], half[1], x, half_done, scalar_grouped)
+                to_quantise[n + 1] = to_quantise.get(n + 1, []) + [(h, r, g, grouped)]
+                if half and half[2]:
+                    to_quantise[n + 2] = [(h, half[0], half[1], scalar_grouped)]
+            for chunk in chunks_read(n + LOOKAHEAD):
+                if chunk not in prepared:
+                    prepare_chunk(*chunk)
+                    prepared.append(chunk)
+            if 0 <= n < len(rounds):
                 if n == 0:
                     for key_chunk in range(N_CHUNKS):
                         regroup_v(0, key_chunk)
-                if r == N_CHUNKS - 1 and h + 1 < HEADS:
-                    regroup_v(h + 1, g)
-                if (r, g) == (1, 0):
+                if half is None and h + 1 < HEADS:
+                    for key_chunk in range(N_CHUNKS):
+                        regroup_v(h + 1, key_chunk)
+                if (r, g) == (1, 1):
                     quantise_v(h)
-            if 1 <= n <= len(batches):
-                quantise_scores(*batches[n - 1], p_grouped[n - 1])
-            if n >= 2:
-                h, r, g = batches[n - 2]
-                if g == r:
-                    weighted_values(h, r)
+            for chunk in complete:
+                weighted_values(*chunk)
+            complete = []
+            for h, r, g, tile_to_quantise in to_quantise.get(n, []):
+                quantise_scores(h, r, g, tile_to_quantise)
+                batches_left[h, r] -= 1
+                if batches_left[h, r] == 0:
+                    complete.append((h, r))

@@ -41,8 +41,8 @@ def tile_model_pa_kernel(tc, q_scaled, k, v, out):
         per_head = ctx.enter_context(tc.tile_pool(name="per_head", bufs=2))
         per_chunk = ctx.enter_context(tc.tile_pool(name="per_chunk", bufs=3))
         work = ctx.enter_context(tc.tile_pool(name="work", bufs=3))
-        psum_vector = ctx.enter_context(tc.psum_pool(name="psum_vector", bufs=3))
-        psum_scalar = ctx.enter_context(tc.psum_pool(name="psum_scalar", bufs=5))
+        psum_vector = ctx.enter_context(tc.psum_pool(name="psum_vector", bufs=4))
+        psum_scalar = ctx.enter_context(tc.psum_pool(name="psum_scalar", bufs=4))
 
         def load(rows, source, h, first_block, n_blocks):
             nc.sync.dma_start(
@@ -125,9 +125,13 @@ def tile_model_pa_kernel(tc, q_scaled, k, v, out):
             transpose_chunk(q_raw[h], q_t[h], c)
 
         def regroup_v(h, g):
-            nc.scalar.copy(
+            nc.gpsimd.tensor_scalar(
                 out=v_grouped[h][:, g, :, :],
-                in_=v_raw[h][:, PACK * g : PACK * (g + 1), :].rearrange("p t d -> p d t"),
+                in0=v_raw[h][:, PACK * g : PACK * (g + 1), :].rearrange("p t d -> p d t"),
+                scalar1=1.0,
+                scalar2=0.0,
+                op0=MULT,
+                op1=mybir.AluOpType.add,
             )
 
         def quantise_v(h):

@@ -24,8 +24,12 @@ N_CHUNKS = SEQ // CHUNK
 BLOCKS = SEQ // P
 
 SHIFT = (PACK - 1) * P
-N_DISTANCES = BLOCKS - PACK
-LOOKAHEAD = 2
+
+KEY_BLOCKS_OF_BANK = ((0,), (1,), (2, 3))
+QUERY_BLOCKS_OF_BANK = ((3,), (2,), (1, 0))
+BANKS = len(KEY_BLOCKS_OF_BANK) + len(QUERY_BLOCKS_OF_BANK)
+
+LAG = PACK
 
 FLOPS = 2 * 2 * HEADS * D * sum(CHUNK * CHUNK * (r + 1) for r in range(N_CHUNKS))
 
@@ -39,18 +43,10 @@ def tile_model_pa_kernel(tc, q_scaled, k, v, out):
         const = ctx.enter_context(tc.tile_pool(name="const", bufs=1))
         raw = ctx.enter_context(tc.tile_pool(name="raw", bufs=HEADS))
         per_head = ctx.enter_context(tc.tile_pool(name="per_head", bufs=2))
-        per_chunk = ctx.enter_context(tc.tile_pool(name="per_chunk", bufs=3))
+        per_chunk = ctx.enter_context(tc.tile_pool(name="per_chunk", bufs=4))
         work = ctx.enter_context(tc.tile_pool(name="work", bufs=3))
         psum_vector = ctx.enter_context(tc.psum_pool(name="psum_vector", bufs=4))
         psum_scalar = ctx.enter_context(tc.psum_pool(name="psum_scalar", bufs=4))
-
-        def load(rows, source, h, first_block, n_blocks):
-            nc.sync.dma_start(
-                out=rows[:, first_block : first_block + n_blocks, :],
-                in_=source[0, h, first_block * P : (first_block + n_blocks) * P, :].rearrange(
-                    "(b p) d -> p b d", p=P
-                ),
-            )
 
         k_raw, q_raw, v_raw = [], [], []
         for h in range(HEADS):
@@ -58,10 +54,11 @@ def tile_model_pa_kernel(tc, q_scaled, k, v, out):
             q_raw.append(raw.tile([P, BLOCKS, D], BF16, name="q_raw"))
             v_raw.append(raw.tile([P, BLOCKS, D], BF16, name="v_raw"))
             for c in range(N_CHUNKS):
-                load(k_raw[h], k, h, PACK * c, PACK)
-                load(q_raw[h], q_scaled, h, PACK * c, PACK)
-                if c == 1:
-                    load(v_raw[h], v, h, 0, BLOCKS)
+                for rows, source in ((k_raw[h], k), (q_raw[h], q_scaled), (v_raw[h], v)):
+                    nc.sync.dma_start(
+                        out=rows[:, PACK * c : PACK * (c + 1), :],
+                        in_=source[0, h, CHUNK * c : CHUNK * (c + 1), :].rearrange("(b p) d -> p b d", p=P),
+                    )
 
         def exponents(shape, pattern, base, channel_multiplier, label):
             as_i32 = const.tile(shape, I32, name=label + "_i32")
@@ -70,12 +67,11 @@ def tile_model_pa_kernel(tc, q_scaled, k, v, out):
             nc.vector.tensor_copy(out=as_f32[:], in_=as_i32[:])
             return as_f32
 
-        table_pattern = [[1, P], [-P, PACK]]
-        table_exponent = exponents([P, P, PACK], table_pattern, SHIFT, -1, "table_exponent")
-        query_exponent = exponents([P, PACK], [[-P, PACK]], SHIFT, 1, "query_exponent")
-        key_exponent = exponents([P, N_DISTANCES], [[P, N_DISTANCES]], P, -1, "key_exponent")
+        table_exponent = exponents([P, P, PACK], [[1, P], [-P, PACK]], SHIFT, -1, "table_exponent")
         identity = const.tile([P, P], BF16)
         make_identity(nc, identity[:])
+        query_exponent = exponents([P, PACK], [[-P, PACK]], SHIFT, 1, "query_exponent")
+        key_exponent = exponents([P, PACK], [[P, PACK]], -SHIFT, -1, "key_exponent")
         identity_f32 = const.tile([P, P], F32)
         make_identity(nc, identity_f32[:])
         diagonal_tiles = []
@@ -84,16 +80,8 @@ def tile_model_pa_kernel(tc, q_scaled, k, v, out):
             nc.vector.memset(zeroed[:], 0.0)
             diagonal_tiles.append(zeroed)
 
-        k_t, q_t, decay, causal, query_factor, key_factor = {}, {}, {}, {}, {}, {}
+        k_t, q_t, decay, query_factor, key_factor = {}, {}, {}, {}, {}
         v_grouped, v_codes, v_scales, p_codes, p_scales = {}, {}, {}, {}, {}
-
-        def transpose_chunk(rows, transposed, c):
-            flipped = psum_scalar.tile([P, PACK, P], BF16, tag="bank")
-            for b in range(PACK):
-                nc.tensor.transpose(out=flipped[:, b, :], in_=rows[:, PACK * c + b, :], identity=identity[:])
-            nc.scalar.copy(
-                out=transposed[:, c * CHUNK : (c + 1) * CHUNK], in_=flipped[:].rearrange("p b x -> p (b x)")
-            )
 
         def power_of_gamma(h, exponent, label):
             power = per_head.tile(list(exponent.shape), F32, name=label)
@@ -104,18 +92,18 @@ def tile_model_pa_kernel(tc, q_scaled, k, v, out):
             k_t[h] = per_head.tile([P, SEQ], BF16, name="k_t")
             q_t[h] = per_head.tile([P, SEQ], BF16, name="q_t")
             v_grouped[h] = per_head.tile([P, N_CHUNKS, D, PACK], BF16, name="v_grouped", align_bytes=64)
+            v_codes[h] = per_head.tile([P, N_CHUNKS, D], U32, name="v_codes", align_bytes=64)
+            v_scales[h] = per_head.tile([P, N_CHUNKS, D], U8, name="v_scales", align_bytes=64)
             decay[h] = power_of_gamma(h, table_exponent, "decay")
             query_factor[h] = power_of_gamma(h, query_exponent, "query_factor")
             key_factor[h] = power_of_gamma(h, key_exponent, "key_factor")
-            causal[h] = per_head.tile([P, P, PACK], F32, name="causal")
-            nc.gpsimd.affine_select(
-                out=causal[h][:],
-                in_=decay[h][:],
-                pattern=table_pattern,
-                compare_op=mybir.AluOpType.is_ge,
-                fill=0.0,
-                base=SHIFT,
-                channel_multiplier=-1,
+
+        def transpose_chunk(rows, transposed, c):
+            flipped = psum_scalar.tile([P, PACK, P], BF16, tag="bank")
+            for b in range(PACK):
+                nc.tensor.transpose(out=flipped[:, b, :], in_=rows[:, PACK * c + b, :], identity=identity[:])
+            nc.scalar.copy(
+                out=transposed[:, c * CHUNK : (c + 1) * CHUNK], in_=flipped[:].rearrange("p b x -> p (b x)")
             )
 
         def prepare_chunk(h, c):
@@ -123,24 +111,20 @@ def tile_model_pa_kernel(tc, q_scaled, k, v, out):
                 start_head(h)
             transpose_chunk(k_raw[h], k_t[h], c)
             transpose_chunk(q_raw[h], q_t[h], c)
-
-        def regroup_v(h, g):
             nc.gpsimd.tensor_scalar(
-                out=v_grouped[h][:, g, :, :],
-                in0=v_raw[h][:, PACK * g : PACK * (g + 1), :].rearrange("p t d -> p d t"),
+                out=v_grouped[h][:, c, :, :],
+                in0=v_raw[h][:, PACK * c : PACK * (c + 1), :].rearrange("p t d -> p d t"),
                 scalar1=1.0,
                 scalar2=0.0,
                 op0=MULT,
                 op1=mybir.AluOpType.add,
             )
 
-        def quantise_v(h):
-            v_codes[h] = per_head.tile([P, N_CHUNKS, D], U32, name="v_codes", align_bytes=64)
-            v_scales[h] = per_head.tile([P, N_CHUNKS, D], U8, name="v_scales", align_bytes=64)
+        def quantise_v(h, c):
             nc.vector.quantize_mx(
-                out=v_codes[h][:].rearrange("p g d -> p (g d)").bitcast(FP8X4),
-                scales=v_scales[h][:].rearrange("p g d -> p (g d)"),
-                in_=v_grouped[h][:].rearrange("p g d t -> p (g d t)"),
+                out=v_codes[h][:, c, :].bitcast(FP8X4),
+                scales=v_scales[h][:, c, :],
+                in_=v_grouped[h][:, c, :, :].rearrange("p d t -> p (d t)"),
             )
 
         def block(transposed, index):
@@ -148,10 +132,8 @@ def tile_model_pa_kernel(tc, q_scaled, k, v, out):
 
 
         def vector_block(h, r, g, b, grouped):
-            diagonal = g == r
-            key_blocks = b + 1 if diagonal else PACK
             scores_t = psum_vector.tile([P, PACK, P], F32)
-            for t in range(key_blocks):
+            for t in range(PACK):
                 nc.tensor.matmul(
                     out=scores_t[:, t, :],
                     lhsT=block(k_t[h], PACK * g + t),
@@ -159,46 +141,64 @@ def tile_model_pa_kernel(tc, q_scaled, k, v, out):
                     start=True,
                     stop=True,
                 )
-            if diagonal:
-                table = causal[h][:, :, PACK - key_blocks : PACK]
-                factor = 1.0
-            else:
-                table = decay[h][:]
-                factor = gammas[h] ** (CHUNK * (r - g) + P * b - SHIFT)
+            distance = CHUNK * (r - g) + P * b
             nc.vector.scalar_tensor_tensor(
-                out=grouped[:, b, :, 0:key_blocks],
-                in0=scores_t[:, 0:key_blocks, :].rearrange("p t i -> p i t"),
-                scalar=factor,
-                in1=table,
+                out=grouped[:, b, :, :],
+                in0=scores_t[:].rearrange("p t i -> p i t"),
+                scalar=gammas[h] ** (distance - SHIFT),
+                in1=decay[h][:],
                 op0=MULT,
                 op1=MULT,
             )
 
-        def scalar_first_half(h, r, g, t, half_done):
+        def by_key_block(h, r, key_blocks, half_done):
             scores = psum_scalar.tile([P, PACK, P], F32, tag="bank")
-            for b in range(PACK):
-                nc.tensor.matmul(
-                    out=scores[:, b, :],
-                    lhsT=block(q_t[h], PACK * r + b),
-                    rhs=block(k_t[h], PACK * g + t),
-                    start=True,
-                    stop=True,
+            first = {}
+            filled = 0
+            for t in key_blocks:
+                first[t] = filled
+                for b in range(t, PACK):
+                    nc.tensor.matmul(
+                        out=scores[:, filled, :],
+                        lhsT=block(q_t[h], PACK * r + b),
+                        rhs=block(k_t[h], PACK * r + t),
+                        start=True,
+                        stop=True,
+                    )
+                    filled += 1
+            for t in key_blocks:
+                nc.scalar.activation(
+                    out=half_done[:, t, t:PACK, :],
+                    in_=scores[:, first[t] : first[t] + PACK - t, :],
+                    func=COPY,
+                    scale=query_factor[h][:, t : t + 1],
                 )
-            nc.scalar.activation(
-                out=half_done[:, t, :, :], in_=scores[:], func=COPY, scale=query_factor[h][:, t : t + 1]
-            )
+                nc.gpsimd.affine_select(
+                    out=half_done[:, t, t, :],
+                    in_=half_done[:, t, t, :],
+                    pattern=[[-1, P]],
+                    compare_op=mybir.AluOpType.is_ge,
+                    fill=0.0,
+                    base=0,
+                    channel_multiplier=1,
+                )
 
-        def scalar_second_half(h, r, g, b, half_done, grouped):
+        def by_query_block(h, query_blocks, half_done, grouped):
             flipped = psum_scalar.tile([P, PACK, P], F32, tag="bank")
-            for t in range(PACK):
-                nc.tensor.transpose(out=flipped[:, t, :], in_=half_done[:, t, b, :], identity=identity_f32[:])
-            m = PACK * (r - g) + b - PACK
-            nc.scalar.activation(
-                out=grouped[:, b, :, :],
-                in_=flipped[:].rearrange("p t i -> p i t"),
-                func=COPY,
-                scale=key_factor[h][:, m : m + 1],
-            )
+            first = {}
+            filled = 0
+            for b in query_blocks:
+                first[b] = filled
+                for t in range(b + 1):
+                    nc.tensor.transpose(out=flipped[:, filled, :], in_=half_done[:, t, b, :], identity=identity_f32[:])
+                    filled += 1
+            for b in query_blocks:
+                nc.scalar.activation(
+                    out=grouped[:, b, :, 0 : b + 1],
+                    in_=flipped[:, first[b] : first[b] + b + 1, :].rearrange("p t i -> p i t"),
+                    func=COPY,
+                    scale=key_factor[h][:, b : b + 1],
+                )
 
         def quantise_scores(h, r, g, grouped):
             if (h, r) not in p_codes:
@@ -230,62 +230,44 @@ def tile_model_pa_kernel(tc, q_scaled, k, v, out):
                 out=out[0, h, r * CHUNK : (r + 1) * CHUNK, :].rearrange("(b p) d -> p b d", p=P), in_=result[:]
             )
 
-        rounds = []
-        for h in range(HEADS):
-            for_vector = [(r, g) for r in range(N_CHUNKS) for g in range(r + 1) if g > 0 or r == 0]
-            for_scalar = [(r, g) for r in range(N_CHUNKS) for g in range(r + 1) if g == 0 and r > 0]
-            halves = [(r, g, second) for (r, g) in for_scalar for second in (False, True)] + [None]
-            rounds.extend((h, batch, half) for batch, half in zip(for_vector, halves))
-
-        def chunks_read(n):
-            if n >= len(rounds):
-                return []
-            h, (r, g), half = rounds[n]
-            return [(h, c) for c in sorted({r, g} | (set(half[0:2]) if half else set()))]
-
-        prepared = []
+        vector_blocks = [
+            (h, r, g, b) for h in range(HEADS) for r in range(N_CHUNKS) for g in range(r) for b in range(PACK)
+        ]
+        chunks = [(h, r) for h in range(HEADS) for r in range(N_CHUNKS)]
+        first_trip = len(KEY_BLOCKS_OF_BANK)
         to_quantise = {}
-        batches_left = {(h, r): r + 1 for h in range(HEADS) for r in range(N_CHUNKS)}
-        complete = []
-        half_done = None
-        scalar_grouped = None
-        for n in range(-LOOKAHEAD, len(rounds) + 3):
-            if 0 <= n < len(rounds):
-                h, (r, g), half = rounds[n]
-                if g == r:
-                    grouped = diagonal_tiles[r % 2]
-                else:
+        to_multiply = {}
+        batches_left = {(h, r): r + 1 for (h, r) in chunks}
+        half_done = {}
+        grouped = None
+        for step in range(-2 * BANKS, len(vector_blocks) + 2 * LAG + 1):
+            if 0 <= step < len(vector_blocks):
+                h, r, g, b = vector_blocks[step]
+                if b == 0:
                     grouped = work.tile([P, PACK, P, PACK], BF16, name="grouped", align_bytes=64)
-                if half and not half[2]:
-                    half_done = work.tile([P, PACK, PACK, P], F32, name="half_done", bufs=2)
-                    scalar_grouped = work.tile([P, PACK, P, PACK], BF16, name="scalar_grouped", align_bytes=64)
-                for x in range(PACK):
-                    vector_block(h, r, g, x, grouped)
-                    if half and not half[2]:
-                        scalar_first_half(h, half[0], half[1], x, half_done)
-                    if half and half[2]:
-                        scalar_second_half(h, half[0], half[1], x, half_done, scalar_grouped)
-                to_quantise[n + 1] = to_quantise.get(n + 1, []) + [(h, r, g, grouped)]
-                if half and half[2]:
-                    to_quantise[n + 2] = [(h, half[0], half[1], scalar_grouped)]
-            for chunk in chunks_read(n + LOOKAHEAD):
-                if chunk not in prepared:
-                    prepare_chunk(*chunk)
-                    prepared.append(chunk)
-            if 0 <= n < len(rounds):
-                if n == 0:
-                    for key_chunk in range(N_CHUNKS):
-                        regroup_v(0, key_chunk)
-                if half is None and h + 1 < HEADS:
-                    for key_chunk in range(N_CHUNKS):
-                        regroup_v(h + 1, key_chunk)
-                if (r, g) == (1, 1):
-                    quantise_v(h)
-            for chunk in complete:
+                vector_block(h, r, g, b, grouped)
+                if b == PACK - 1:
+                    to_quantise[step + LAG] = to_quantise.get(step + LAG, []) + [(h, r, g, grouped)]
+
+            y, bank = divmod(step + BANKS, BANKS)
+            if bank == 0 and 0 <= y + 1 < len(chunks):
+                prepare_chunk(*chunks[y + 1])
+            if bank == first_trip and 0 <= y + 1 < len(chunks):
+                quantise_v(*chunks[y + 1])
+            if bank < first_trip and 0 <= y < len(chunks):
+                if bank == 0:
+                    half_done[y] = work.tile([P, PACK, PACK, P], F32, name="half_done", bufs=2)
+                by_key_block(*chunks[y], KEY_BLOCKS_OF_BANK[bank], half_done[y])
+            if bank >= first_trip and 0 <= y - 1 < len(chunks):
+                h, r = chunks[y - 1]
+                by_query_block(h, QUERY_BLOCKS_OF_BANK[bank - first_trip], half_done[y - 1], diagonal_tiles[y % 2])
+                if bank == BANKS - 1:
+                    to_quantise[step + LAG] = to_quantise.get(step + LAG, []) + [(h, r, r, diagonal_tiles[y % 2])]
+
+            for chunk in to_multiply.get(step, []):
                 weighted_values(*chunk)
-            complete = []
-            for h, r, g, tile_to_quantise in to_quantise.get(n, []):
-                quantise_scores(h, r, g, tile_to_quantise)
+            for h, r, g, written in to_quantise.get(step, []):
+                quantise_scores(h, r, g, written)
                 batches_left[h, r] -= 1
                 if batches_left[h, r] == 0:
-                    complete.append((h, r))
+                    to_multiply[step + LAG] = to_multiply.get(step + LAG, []) + [(h, r)]

@@ -29,6 +29,7 @@ KEY_BLOCKS_OF_BANK = ((0,), (1,), (2, 3))
 QUERY_BLOCKS_OF_BANK = ((3,), (2,), (1, 0))
 BANKS = len(KEY_BLOCKS_OF_BANK) + len(QUERY_BLOCKS_OF_BANK)
 
+LOADS_AHEAD = 2 * N_CHUNKS
 LAG = PACK
 
 FLOPS = 2 * 2 * HEADS * D * sum(CHUNK * CHUNK * (r + 1) for r in range(N_CHUNKS))
@@ -41,24 +42,29 @@ def tile_model_pa_kernel(tc, q_scaled, k, v, out):
     with ExitStack() as ctx:
         ctx.enter_context(tc.manual_schedule())
         const = ctx.enter_context(tc.tile_pool(name="const", bufs=1))
-        raw = ctx.enter_context(tc.tile_pool(name="raw", bufs=HEADS))
+        raw = ctx.enter_context(tc.tile_pool(name="raw", bufs=LOADS_AHEAD // N_CHUNKS + 2))
         per_head = ctx.enter_context(tc.tile_pool(name="per_head", bufs=2))
-        per_chunk = ctx.enter_context(tc.tile_pool(name="per_chunk", bufs=4))
+        per_chunk = ctx.enter_context(tc.tile_pool(name="per_chunk", bufs=5))
         work = ctx.enter_context(tc.tile_pool(name="work", bufs=3))
         psum_vector = ctx.enter_context(tc.psum_pool(name="psum_vector", bufs=4))
         psum_scalar = ctx.enter_context(tc.psum_pool(name="psum_scalar", bufs=4))
 
-        k_raw, q_raw, v_raw = [], [], []
-        for h in range(HEADS):
-            k_raw.append(raw.tile([P, BLOCKS, D], BF16, name="k_raw"))
-            q_raw.append(raw.tile([P, BLOCKS, D], BF16, name="q_raw"))
-            v_raw.append(raw.tile([P, BLOCKS, D], BF16, name="v_raw"))
-            for c in range(N_CHUNKS):
-                for rows, source in ((k_raw[h], k), (q_raw[h], q_scaled), (v_raw[h], v)):
-                    nc.sync.dma_start(
-                        out=rows[:, PACK * c : PACK * (c + 1), :],
-                        in_=source[0, h, CHUNK * c : CHUNK * (c + 1), :].rearrange("(b p) d -> p b d", p=P),
-                    )
+        k_raw, q_raw, v_raw = {}, {}, {}
+
+        def load_chunk(h, c):
+            if c == 0:
+                k_raw[h] = raw.tile([P, BLOCKS, D], BF16, name="k_raw")
+                q_raw[h] = raw.tile([P, BLOCKS, D], BF16, name="q_raw")
+                v_raw[h] = raw.tile([P, BLOCKS, D], BF16, name="v_raw")
+            for rows, source in ((k_raw[h], k), (q_raw[h], q_scaled), (v_raw[h], v)):
+                nc.sync.dma_start(
+                    out=rows[:, PACK * c : PACK * (c + 1), :],
+                    in_=source[0, h, CHUNK * c : CHUNK * (c + 1), :].rearrange("(b p) d -> p b d", p=P),
+                )
+
+        chunks = [(h, r) for h in range(HEADS) for r in range(N_CHUNKS)]
+        for chunk in chunks[0:LOADS_AHEAD]:
+            load_chunk(*chunk)
 
         def exponents(shape, pattern, base, channel_multiplier, label):
             as_i32 = const.tile(shape, I32, name=label + "_i32")
@@ -226,21 +232,20 @@ def tile_model_pa_kernel(tc, q_scaled, k, v, out):
                     )
             result = work.tile([P, PACK, D], F32)
             nc.scalar.copy(out=result[:], in_=acc[:])
-            nc.gpsimd.dma_start(
+            nc.sync.dma_start(
                 out=out[0, h, r * CHUNK : (r + 1) * CHUNK, :].rearrange("(b p) d -> p b d", p=P), in_=result[:]
             )
 
         vector_blocks = [
             (h, r, g, b) for h in range(HEADS) for r in range(N_CHUNKS) for g in range(r) for b in range(PACK)
         ]
-        chunks = [(h, r) for h in range(HEADS) for r in range(N_CHUNKS)]
         first_trip = len(KEY_BLOCKS_OF_BANK)
         to_quantise = {}
         to_multiply = {}
         batches_left = {(h, r): r + 1 for (h, r) in chunks}
         half_done = {}
         grouped = None
-        for step in range(-2 * BANKS, len(vector_blocks) + 2 * LAG + 1):
+        for step in range(-2 * BANKS, len(vector_blocks) + BANKS + 2 * LAG + 1):
             if 0 <= step < len(vector_blocks):
                 h, r, g, b = vector_blocks[step]
                 if b == 0:
@@ -249,11 +254,13 @@ def tile_model_pa_kernel(tc, q_scaled, k, v, out):
                 if b == PACK - 1:
                     to_quantise[step + LAG] = to_quantise.get(step + LAG, []) + [(h, r, g, grouped)]
 
-            y, bank = divmod(step + BANKS, BANKS)
-            if bank == 0 and 0 <= y + 1 < len(chunks):
-                prepare_chunk(*chunks[y + 1])
-            if bank == first_trip and 0 <= y + 1 < len(chunks):
-                quantise_v(*chunks[y + 1])
+            y, bank = divmod(step, BANKS)
+            if bank == 0 and 0 <= y + 2 < len(chunks):
+                prepare_chunk(*chunks[y + 2])
+                if y + 2 + LOADS_AHEAD < len(chunks):
+                    load_chunk(*chunks[y + 2 + LOADS_AHEAD])
+            if bank == first_trip and 0 <= y < len(chunks):
+                quantise_v(*chunks[y])
             if bank < first_trip and 0 <= y < len(chunks):
                 if bank == 0:
                     half_done[y] = work.tile([P, PACK, PACK, P], F32, name="half_done", bufs=2)

import math
from contextlib import ExitStack

import concourse.mybir as mybir
from concourse.masks import make_identity

BF16 = mybir.dt.bfloat16
F32 = mybir.dt.float32
I32 = mybir.dt.int32
U32 = mybir.dt.uint32
U8 = mybir.dt.uint8
FP8X4 = mybir.dt.float8_e4m3fn_x4
MULT = mybir.AluOpType.mult
COPY = mybir.ActivationFunctionType.Copy
EXP = mybir.ActivationFunctionType.Exp

HEADS = 8
SEQ = 2048
D = 128
P = 128
PACK = 4
CHUNK = P * PACK
N_CHUNKS = SEQ // CHUNK
BLOCKS = SEQ // P

SHIFT = (PACK - 1) * P

KEY_BLOCKS_OF_BANK = ((0,), (1,), (2, 3))
QUERY_BLOCKS_OF_BANK = ((3,), (2,), (1, 0))
BANKS = len(KEY_BLOCKS_OF_BANK) + len(QUERY_BLOCKS_OF_BANK)

LOADS_AHEAD = 2 * N_CHUNKS
LAG = PACK

FLOPS = 2 * 2 * HEADS * D * sum(CHUNK * CHUNK * (r + 1) for r in range(N_CHUNKS))


def tile_model_pa_kernel(tc, q_scaled, k, v, out):
    nc = tc.nc
    gammas = [1.0 - 2.0 ** (-5 - h) for h in range(HEADS)]

    with ExitStack() as ctx:
        ctx.enter_context(tc.manual_schedule())
        const = ctx.enter_context(tc.tile_pool(name="const", bufs=1))
        raw = ctx.enter_context(tc.tile_pool(name="raw", bufs=LOADS_AHEAD // N_CHUNKS + 2))
        per_head = ctx.enter_context(tc.tile_pool(name="per_head", bufs=2))
        per_chunk = ctx.enter_context(tc.tile_pool(name="per_chunk", bufs=5))
        work = ctx.enter_context(tc.tile_pool(name="work", bufs=3))
        psum_vector = ctx.enter_context(tc.psum_pool(name="psum_vector", bufs=4))
        psum_scalar = ctx.enter_context(tc.psum_pool(name="psum_scalar", bufs=4))

        k_raw, q_raw, v_raw = {}, {}, {}

        def load_chunk(h, c):
            if c == 0:
                k_raw[h] = raw.tile([P, BLOCKS, D], BF16, name="k_raw")
                q_raw[h] = raw.tile([P, BLOCKS, D], BF16, name="q_raw")
                v_raw[h] = raw.tile([P, BLOCKS, D], BF16, name="v_raw")
            for rows, source in ((k_raw[h], k), (q_raw[h], q_scaled), (v_raw[h], v)):
                nc.sync.dma_start(
                    out=rows[:, PACK * c : PACK * (c + 1), :],
                    in_=source[0, h, CHUNK * c : CHUNK * (c + 1), :].rearrange("(b p) d -> p b d", p=P),
                )

        chunks = [(h, r) for h in range(HEADS) for r in range(N_CHUNKS)]
        for chunk in chunks[0:LOADS_AHEAD]:
            load_chunk(*chunk)

        def exponents(shape, pattern, base, channel_multiplier, label):
            as_i32 = const.tile(shape, I32, name=label + "_i32")
            nc.gpsimd.iota(as_i32[:], pattern=pattern, base=base, channel_multiplier=channel_multiplier)
            as_f32 = const.tile(shape, F32, name=label)
            nc.vector.tensor_copy(out=as_f32[:], in_=as_i32[:])
            return as_f32

        table_exponent = exponents([P, P, PACK], [[1, P], [-P, PACK]], SHIFT, -1, "table_exponent")
        identity = const.tile([P, P], BF16)
        make_identity(nc, identity[:])
        query_exponent = exponents([P, PACK], [[-P, PACK]], SHIFT, 1, "query_exponent")
        key_exponent = exponents([P, PACK], [[P, PACK]], -SHIFT, -1, "key_exponent")
        identity_f32 = const.tile([P, P], F32)
        make_identity(nc, identity_f32[:])
        diagonal_tiles = []
        for i in range(2):
            zeroed = const.tile([P, PACK, P, PACK], BF16, name="diagonal%d" % i, align_bytes=64)
            nc.vector.memset(zeroed[:], 0.0)
            diagonal_tiles.append(zeroed)

        k_t, q_t, decay, query_factor, key_factor = {}, {}, {}, {}, {}
        v_grouped, v_codes, v_scales, p_codes, p_scales = {}, {}, {}, {}, {}

        def power_of_gamma(h, exponent, label):
            power = per_head.tile(list(exponent.shape), F32, name=label)
            nc.scalar.activation(out=power[:], in_=exponent[:], func=EXP, scale=math.log(gammas[h]))
            return power

        def start_head(h):
            k_t[h] = per_head.tile([P, SEQ], BF16, name="k_t")
            q_t[h] = per_head.tile([P, SEQ], BF16, name="q_t")
            v_grouped[h] = per_head.tile([P, N_CHUNKS, D, PACK], BF16, name="v_grouped", align_bytes=64)
            v_codes[h] = per_head.tile([P, N_CHUNKS, D], U32, name="v_codes", align_bytes=64)
            v_scales[h] = per_head.tile([P, N_CHUNKS, D], U8, name="v_scales", align_bytes=64)
            decay[h] = power_of_gamma(h, table_exponent, "decay")
            query_factor[h] = power_of_gamma(h, query_exponent, "query_factor")
            key_factor[h] = power_of_gamma(h, key_exponent, "key_factor")

        def transpose_chunk(rows, transposed, c):
            flipped = psum_scalar.tile([P, PACK, P], BF16, tag="bank")
            for b in range(PACK):
                nc.tensor.transpose(out=flipped[:, b, :], in_=rows[:, PACK * c + b, :], identity=identity[:])
            nc.scalar.copy(
                out=transposed[:, c * CHUNK : (c + 1) * CHUNK], in_=flipped[:].rearrange("p b x -> p (b x)")
            )

        def prepare_chunk(h, c):
            if c == 0:
                start_head(h)
            transpose_chunk(k_raw[h], k_t[h], c)
            transpose_chunk(q_raw[h], q_t[h], c)
            nc.gpsimd.tensor_scalar(
                out=v_grouped[h][:, c, :, :],
                in0=v_raw[h][:, PACK * c : PACK * (c + 1), :].rearrange("p t d -> p d t"),
                scalar1=1.0,
                scalar2=0.0,
                op0=MULT,
                op1=mybir.AluOpType.add,
            )

        def quantise_v(h, c):
            nc.vector.quantize_mx(
                out=v_codes[h][:, c, :].bitcast(FP8X4),
                scales=v_scales[h][:, c, :],
                in_=v_grouped[h][:, c, :, :].rearrange("p d t -> p (d t)"),
            )

        def block(transposed, index):
            return transposed[:, index * P : (index + 1) * P]


        def vector_block(h, r, g, b, grouped):
            scores_t = psum_vector.tile([P, PACK, P], F32)
            for t in range(PACK):
                nc.tensor.matmul(
                    out=scores_t[:, t, :],
                    lhsT=block(k_t[h], PACK * g + t),
                    rhs=block(q_t[h], PACK * r + b),
                    start=True,
                    stop=True,
                )
            distance = CHUNK * (r - g) + P * b
            nc.vector.scalar_tensor_tensor(
                out=grouped[:, b, :, :],
                in0=scores_t[:].rearrange("p t i -> p i t"),
                scalar=gammas[h] ** (distance - SHIFT),
                in1=decay[h][:],
                op0=MULT,
                op1=MULT,
            )

        def by_key_block(h, r, key_blocks, half_done):
            scores = psum_scalar.tile([P, PACK, P], F32, tag="bank")
            first = {}
            filled = 0
            for t in key_blocks:
                first[t] = filled
                for b in range(t, PACK):
                    nc.tensor.matmul(
                        out=scores[:, filled, :],
                        lhsT=block(q_t[h], PACK * r + b),
                        rhs=block(k_t[h], PACK * r + t),
                        start=True,
                        stop=True,
                    )
                    filled += 1
            for t in key_blocks:
                nc.scalar.activation(
                    out=half_done[:, t, t:PACK, :],
                    in_=scores[:, first[t] : first[t] + PACK - t, :],
                    func=COPY,
                    scale=query_factor[h][:, t : t + 1],
                )
                nc.gpsimd.affine_select(
                    out=half_done[:, t, t, :],
                    in_=half_done[:, t, t, :],
                    pattern=[[-1, P]],
                    compare_op=mybir.AluOpType.is_ge,
                    fill=0.0,
                    base=0,
                    channel_multiplier=1,
                )

        def by_query_block(h, query_blocks, half_done, grouped):
            flipped = psum_scalar.tile([P, PACK, P], F32, tag="bank")
            first = {}
            filled = 0
            for b in query_blocks:
                first[b] = filled
                for t in range(b + 1):
                    nc.tensor.transpose(out=flipped[:, filled, :], in_=half_done[:, t, b, :], identity=identity_f32[:])
                    filled += 1
            for b in query_blocks:
                nc.scalar.activation(
                    out=grouped[:, b, :, 0 : b + 1],
                    in_=flipped[:, first[b] : first[b] + b + 1, :].rearrange("p t i -> p i t"),
                    func=COPY,
                    scale=key_factor[h][:, b : b + 1],
                )

        def quantise_scores(h, r, g, grouped):
            if (h, r) not in p_codes:
                p_codes[h, r] = per_chunk.tile([P, N_CHUNKS, CHUNK], U32, name="p_codes", align_bytes=64)
                p_scales[h, r] = per_chunk.tile([P, N_CHUNKS, CHUNK], U8, name="p_scales", align_bytes=64)
            nc.vector.quantize_mx(
                out=p_codes[h, r][:, g, :].bitcast(FP8X4),
                scales=p_scales[h, r][:, g, :],
                in_=grouped[:].rearrange("p b i t -> p (b i t)"),
            )

        def weighted_values(h, r):
            acc = psum_scalar.tile([P, PACK, D], F32, tag="bank")
            for b in range(PACK):
                queries = slice(b * P, (b + 1) * P)
                for g in range(r + 1):
                    nc.tensor.matmul_mx(
                        out=acc[:, b, :],
                        lhsT=p_codes[h, r][:, g, queries].bitcast(FP8X4),
                        lhsT_scale=p_scales[h, r][:, g, queries],
                        rhs=v_codes[h][:, g, :].bitcast(FP8X4),
                        rhs_scale=v_scales[h][:, g, :],
                        start=(g == 0),
                        stop=(g == r),
                    )
            result = work.tile([P, PACK, D], F32)
            nc.scalar.copy(out=result[:], in_=acc[:])
            nc.sync.dma_start(
                out=out[0, h, r * CHUNK : (r + 1) * CHUNK, :].rearrange("(b p) d -> p b d", p=P), in_=result[:]
            )

        vector_blocks = [
            (h, r, g, b) for h in range(HEADS) for r in range(N_CHUNKS) for g in range(r) for b in range(PACK)
        ]
        first_trip = len(KEY_BLOCKS_OF_BANK)
        to_quantise = {}
        to_multiply = {}
        batches_left = {(h, r): r + 1 for (h, r) in chunks}
        half_done = {}
        grouped = None
        for step in range(-2 * BANKS, len(vector_blocks) + BANKS + 2 * LAG + 1):
            if 0 <= step < len(vector_blocks):
                h, r, g, b = vector_blocks[step]
                if b == 0:
                    grouped = work.tile([P, PACK, P, PACK], BF16, name="grouped", align_bytes=64)
                vector_block(h, r, g, b, grouped)
                if b == PACK - 1:
                    to_quantise[step + LAG] = to_quantise.get(step + LAG, []) + [(h, r, g, grouped)]

            y, bank = divmod(step, BANKS)
            if bank == 0 and 0 <= y + 2 < len(chunks):
                prepare_chunk(*chunks[y + 2])
                if y + 2 + LOADS_AHEAD < len(chunks):
                    load_chunk(*chunks[y + 2 + LOADS_AHEAD])
            if bank == first_trip and 0 <= y < len(chunks):
                quantise_v(*chunks[y])
            if bank < first_trip and 0 <= y < len(chunks):
                if bank == 0:
                    half_done[y] = work.tile([P, PACK, PACK, P], F32, name="half_done", bufs=2)
                by_key_block(*chunks[y], KEY_BLOCKS_OF_BANK[bank], half_done[y])
            if bank >= first_trip and 0 <= y - 1 < len(chunks):
                h, r = chunks[y - 1]
                by_query_block(h, QUERY_BLOCKS_OF_BANK[bank - first_trip], half_done[y - 1], diagonal_tiles[y % 2])
                if bank == BANKS - 1:
                    to_quantise[step + LAG] = to_quantise.get(step + LAG, []) + [(h, r, r, diagonal_tiles[y % 2])]

            for chunk in to_multiply.get(step, []):
                weighted_values(*chunk)
            for h, r, g, written in to_quantise.get(step, []):
                quantise_scores(h, r, g, written)
                batches_left[h, r] -= 1
                if batches_left[h, r] == 0:
                    to_multiply[step + LAG] = to_multiply.get(step + LAG, []) + [(h, r)]
